import numpy as np
import ml_dtypes


def mxq(x, axis, fmt="e4m3"):
    dtype, down = {"e4m3": (ml_dtypes.float8_e4m3fn, 7), "e5m2": (ml_dtypes.float8_e5m2, 14)}[fmt]
    v = np.moveaxis(np.asarray(x, np.float32).astype(ml_dtypes.bfloat16).astype(np.float64), axis, -1)
    blocks = v.reshape(v.shape[:-1] + (-1, 32))
    amax = np.abs(blocks).max(-1, keepdims=True)
    byte = np.maximum(np.where(amax > 0, np.frexp(amax)[1] - 1 + 127, 0) - down, 1)
    scale = np.exp2(byte - 127.0)
    codes = (blocks / scale).astype(np.float32).astype(dtype).astype(np.float64)
    return np.moveaxis((codes * scale).reshape(v.shape), -1, axis)


WIDE = False


def mx_kscale(k):
    if not WIDE:
        return np.ones(k)
    levels = np.array([10, -10, 5, -5, 0])
    a = np.random.permutation(np.resize(levels, k // 512 * 4)).reshape(k // 512, 4)
    idx = np.arange(k)
    return np.exp2(a[idx // 512, idx % 128 // 32])


BF16 = ml_dtypes.bfloat16


def bf(x):
    return np.asarray(x, np.float32).astype(BF16)


def f64(x):
    return np.asarray(x).astype(np.float64)


B, N, C, H = 4, 1024, 512, 16
EPS = 1e-6


def rmsnorm(v, w):
    var = np.mean(np.square(v), axis=-1, keepdims=True)
    return v * (1.0 / np.sqrt(var + EPS)) * w


def setup_inputs():
    s = mx_kscale(C)
    return {"x": bf(np.random.standard_normal((B, N, C)) * s),
            "w_qkv": bf(np.random.standard_normal((3 * C, C)) / np.sqrt(C) / s[None, :]),
            "q_norm_w": bf(1.0 + 0.1 * np.random.standard_normal(C)),
            "k_norm_w": bf(1.0 + 0.1 * np.random.standard_normal(C))}


def reference(x, w_qkv, q_norm_w, k_norm_w):
    xq = mxq(f64(x), 2, "e4m3")
    wt = f64(w_qkv).T
    q = xq @ mxq(wt[:, :C], 0, "e4m3")
    k = xq @ mxq(wt[:, C:2 * C], 0, "e4m3")
    v = xq @ mxq(wt[:, 2 * C:], 0, "e4m3")
    return rmsnorm(q, f64(q_norm_w)), rmsnorm(k, f64(k_norm_w)), v

@@ -1,0 +1,212 @@
+from contextlib import ExitStack
+
+import concourse.mybir as mybir
+from concourse.masks import make_identity
+
+F32 = mybir.dt.float32
+BF16 = mybir.dt.bfloat16
+U32 = mybir.dt.uint32
+U8 = mybir.dt.uint8
+FP8X4 = mybir.dt.float8_e4m3fn_x4
+ACT = mybir.ActivationFunctionType
+ALU = mybir.AluOpType
+
+P = 128
+HIDDEN = 512
+TOKENS = 4 * 1024
+TILES = TOKENS // P
+BLOCKS = 4
+GROUPS = TILES // BLOCKS
+STORED = 2
+WORDS = HIDDEN // 2
+EPS = 1e-6
+FLIP_AHEAD = 4
+QUANT_AHEAD = 3
+
+FLOPS = 2 * TOKENS * HIDDEN * 3 * HIDDEN
+
+
+def tile_internattention_pa_t_kernel(
+    tc, x, w_qkv, q_norm_w, k_norm_w, out_0, out_1, out_2
+):
+    nc = tc.nc
+    with ExitStack() as ctx:
+        consts = ctx.enter_context(tc.tile_pool(name="consts", bufs=1))
+        x_pool = ctx.enter_context(tc.tile_pool(name="x_pool", bufs=GROUPS))
+        w_pool = ctx.enter_context(tc.tile_pool(name="w_pool", bufs=3))
+        x_mx_pool = ctx.enter_context(tc.tile_pool(name="x_mx_pool", bufs=FLIP_AHEAD + 2))
+        small = ctx.enter_context(tc.tile_pool(name="small", bufs=4))
+        out_pool = ctx.enter_context(tc.tile_pool(name="out_pool", bufs=8))
+        psum = ctx.enter_context(tc.psum_pool(name="psum", bufs=2))
+        ctx.enter_context(tc.manual_schedule())
+
+        x_rows = x.flatten_outer_dims().rearrange("(p t) k -> p t k", t=TILES)
+        q_rows = out_0.flatten_outer_dims().rearrange("(p t) c -> p t c", t=TILES)
+        k_rows = out_1.flatten_outer_dims().rearrange("(p t) c -> p t c", t=TILES)
+        v_rows = out_2.flatten_outer_dims().rearrange("(p t) c -> p t c", t=TILES)
+        w_rows = w_qkv.rearrange("(j p) k -> p j k", p=P)
+
+        gain_rows = consts.tile([P, 2 * HIDDEN], BF16)
+        nc.vector.memset(gain_rows[:], 0.0)
+        ones = consts.tile([P, P], BF16)
+        nc.vector.memset(ones[:], 1.0)
+        eps = consts.tile([P, 1], F32)
+        nc.vector.memset(eps[:], EPS)
+        ident = consts.tile([P, P], F32)
+        make_identity(nc, ident[:])
+        warm = consts.tile([P, 1], F32)
+        nc.scalar.activation(out=warm[:], in_=eps[:], func=ACT.Sqrt)
+
+        def load(pool, rows):
+            raw = pool.tile([P, BLOCKS * HIDDEN], BF16)
+            nc.sync.dma_start(out=raw[:].rearrange("p (b k) -> p b k", b=BLOCKS), in_=rows)
+            return raw
+
+        x_raw = [load(x_pool, x_rows[:, 0:BLOCKS, :])]
+        w_raw = [load(w_pool, w_rows[:, c * BLOCKS : (c + 1) * BLOCKS, :]) for c in range(3)]
+        nc.sync.dma_start(out=gain_rows[0:1, 0:HIDDEN], in_=q_norm_w.unsqueeze(0))
+        nc.sync.dma_start(out=gain_rows[0:1, HIDDEN : 2 * HIDDEN], in_=k_norm_w.unsqueeze(0))
+        for g in range(1, GROUPS):
+            x_raw.append(load(x_pool, x_rows[:, g * BLOCKS : (g + 1) * BLOCKS, :]))
+
+        def flip(raw_words, grouped_words, blocks, copy):
+            flipped = psum.tile([P, blocks * WORDS], F32)
+            for b in range(blocks):
+                for u in range(2):
+                    nc.tensor.transpose(
+                        out=flipped[:, (2 * b + u) * P : (2 * b + u + 1) * P],
+                        in_=raw_words[:, b * WORDS + u * P : b * WORDS + (u + 1) * P],
+                        identity=ident[:],
+                    )
+            copy(
+                out=grouped_words.rearrange("p (b r u) -> p b r u", b=blocks, u=2),
+                in_=flipped[:].rearrange("p (b u r) -> p b r u", b=blocks, u=2),
+            )
+
+        x_grouped = []
+        x_mx = []
+
+        def flip_x(n):
+            g, b = divmod(n, BLOCKS)
+            grouped = x_mx_pool.tile([P, HIDDEN], BF16, align_bytes=64)
+            flip(
+                x_raw[g][:].bitcast(F32)[:, b * WORDS : (b + 1) * WORDS],
+                grouped[:].bitcast(F32),
+                1,
+                nc.vector.tensor_copy,
+            )
+            x_grouped.append(grouped)
+
+        def quantise_x(n):
+            x_codes = x_mx_pool.tile([P, P], U32, align_bytes=64)
+            x_scales = x_mx_pool.tile([P, P], U8, align_bytes=64)
+            nc.vector.quantize_mx(
+                out=x_codes[:].bitcast(FP8X4), scales=x_scales[:], in_=x_grouped[n][:]
+            )
+            x_mx.append((x_codes, x_scales))
+
+        for n in range(FLIP_AHEAD):
+            flip_x(n)
+        for n in range(QUANT_AHEAD):
+            quantise_x(n)
+
+        w_mx = []
+        for c in range(3):
+            w_grouped = w_pool.tile([P, BLOCKS * HIDDEN], BF16, align_bytes=64)
+            for half in range(2):
+                words = slice(half * 2 * WORDS, (half + 1) * 2 * WORDS)
+                flip(
+                    w_raw[c][:].bitcast(F32)[:, words],
+                    w_grouped[:].bitcast(F32)[:, words],
+                    2,
+                    nc.scalar.copy,
+                )
+            w_codes = w_pool.tile([P, HIDDEN], U32, align_bytes=64)
+            w_scales = w_pool.tile([P, HIDDEN], U8, align_bytes=64)
+            nc.vector.quantize_mx(
+                out=w_codes[:].bitcast(FP8X4), scales=w_scales[:], in_=w_grouped[:]
+            )
+            w_mx.append((w_codes, w_scales))
+
+        gains = consts.tile([P, 2, HIDDEN], F32)
+        for c in range(2):
+            spread = psum.tile([P, HIDDEN], F32, tag="acc_v")
+            nc.tensor.matmul(
+                out=spread[:],
+                lhsT=ones[:],
+                rhs=gain_rows[:, c * HIDDEN : (c + 1) * HIDDEN],
+                start=True,
+                stop=True,
+            )
+            nc.scalar.copy(out=gains[:, c, :], in_=spread[:])
+
+        for n in range(TILES):
+            b = n % STORED
+            if b == 0:
+                q_out = out_pool.tile([P, STORED, HIDDEN], F32)
+                k_out = out_pool.tile([P, STORED, HIDDEN], F32)
+                v_out = out_pool.tile([P, STORED, HIDDEN], F32)
+            x_codes, x_scales = x_mx[n]
+
+            def project(acc, c):
+                nc.tensor.matmul_mx(
+                    out=acc[:],
+                    lhsT=x_codes[:].bitcast(FP8X4),
+                    lhsT_scale=x_scales[:],
+                    rhs=w_mx[c][0][:].bitcast(FP8X4),
+                    rhs_scale=w_mx[c][1][:],
+                    start=True,
+                    stop=True,
+                )
+
+            acc_q = psum.tile([P, HIDDEN], F32)
+            project(acc_q, 0)
+            acc_k = psum.tile([P, HIDDEN], F32)
+            project(acc_k, 1)
+            acc_v = psum.tile([P, HIDDEN], F32)
+            project(acc_v, 2)
+
+            sum_sq = small.tile([P, 2], F32)
+            squares = small.tile([P, HIDDEN], BF16)
+            nc.scalar.activation(
+                out=squares[:], in_=acc_q[:], func=ACT.Square, accum_out=sum_sq[:, 0:1]
+            )
+            squares = small.tile([P, HIDDEN], BF16)
+            nc.scalar.activation(
+                out=squares[:], in_=acc_k[:], func=ACT.Square, accum_out=sum_sq[:, 1:2]
+            )
+            rms = small.tile([P, 2], F32)
+            nc.scalar.activation(
+                out=rms[:], in_=sum_sq[:], func=ACT.Sqrt, scale=1.0 / HIDDEN, bias=eps[:]
+            )
+            nc.scalar.copy(out=v_out[:, b, :], in_=acc_v[:])
+
+            inv_rms = small.tile([P, 2], F32)
+            nc.vector.reciprocal(out=inv_rms[:], in_=rms[:])
+            nc.vector.scalar_tensor_tensor(
+                out=q_out[:, b, :],
+                in0=acc_q[:],
+                scalar=inv_rms[:, 0:1],
+                in1=gains[:, 0, :],
+                op0=ALU.mult,
+                op1=ALU.mult,
+            )
+            nc.vector.scalar_tensor_tensor(
+                out=k_out[:, b, :],
+                in0=acc_k[:],
+                scalar=inv_rms[:, 1:2],
+                in1=gains[:, 1, :],
+                op0=ALU.mult,
+                op1=ALU.mult,
+            )
+
+            if n + FLIP_AHEAD < TILES:
+                flip_x(n + FLIP_AHEAD)
+            if n + QUANT_AHEAD < TILES:
+                quantise_x(n + QUANT_AHEAD)
+
+            if b == STORED - 1:
+                tiles = slice(n + 1 - STORED, n + 1)
+                nc.sync.dma_start(out=v_rows[:, tiles, :], in_=v_out[:])
+                nc.sync.dma_start(out=q_rows[:, tiles, :], in_=q_out[:])
+                nc.sync.dma_start(out=k_rows[:, tiles, :], in_=k_out[:])

@@ -37,7 +37,8 @@ def tile_internattention_pa_t_kernel(
         x_mx_pool = ctx.enter_context(tc.tile_pool(name="x_mx_pool", bufs=FLIP_AHEAD + 2))
         small = ctx.enter_context(tc.tile_pool(name="small", bufs=4))
         out_pool = ctx.enter_context(tc.tile_pool(name="out_pool", bufs=8))
-        psum = ctx.enter_context(tc.psum_pool(name="psum", bufs=2))
+        banks = ctx.enter_context(tc.psum_pool(name="banks", bufs=7))
+        flip_bank = ctx.enter_context(tc.psum_pool(name="flip_bank", bufs=1))
         ctx.enter_context(tc.manual_schedule())
 
         x_rows = x.flatten_outer_dims().rearrange("(p t) k -> p t k", t=TILES)
@@ -54,6 +55,8 @@ def tile_internattention_pa_t_kernel(
         nc.vector.memset(eps[:], EPS)
         ident = consts.tile([P, P], F32)
         make_identity(nc, ident[:])
+        nc.scalar.dma_start(out=gain_rows[0:1, 0:HIDDEN], in_=q_norm_w.unsqueeze(0))
+        nc.scalar.dma_start(out=gain_rows[0:1, HIDDEN : 2 * HIDDEN], in_=k_norm_w.unsqueeze(0))
         warm = consts.tile([P, 1], F32)
         nc.scalar.activation(out=warm[:], in_=eps[:], func=ACT.Sqrt)
 
@@ -64,13 +67,11 @@ def tile_internattention_pa_t_kernel(
 
         x_raw = [load(x_pool, x_rows[:, 0:BLOCKS, :])]
         w_raw = [load(w_pool, w_rows[:, c * BLOCKS : (c + 1) * BLOCKS, :]) for c in range(3)]
-        nc.sync.dma_start(out=gain_rows[0:1, 0:HIDDEN], in_=q_norm_w.unsqueeze(0))
-        nc.sync.dma_start(out=gain_rows[0:1, HIDDEN : 2 * HIDDEN], in_=k_norm_w.unsqueeze(0))
         for g in range(1, GROUPS):
             x_raw.append(load(x_pool, x_rows[:, g * BLOCKS : (g + 1) * BLOCKS, :]))
 
-        def flip(raw_words, grouped_words, blocks, copy):
-            flipped = psum.tile([P, blocks * WORDS], F32)
+        def flip(pool, raw_words, grouped_words, blocks, copy):
+            flipped = pool.tile([P, blocks * WORDS], F32, tag="bank")
             for b in range(blocks):
                 for u in range(2):
                     nc.tensor.transpose(
@@ -86,10 +87,11 @@ def tile_internattention_pa_t_kernel(
         x_grouped = []
         x_mx = []
 
-        def flip_x(n):
+        def flip_x(pool, n):
             g, b = divmod(n, BLOCKS)
             grouped = x_mx_pool.tile([P, HIDDEN], BF16, align_bytes=64)
             flip(
+                pool,
                 x_raw[g][:].bitcast(F32)[:, b * WORDS : (b + 1) * WORDS],
                 grouped[:].bitcast(F32),
                 1,
@@ -106,7 +108,7 @@ def tile_internattention_pa_t_kernel(
             x_mx.append((x_codes, x_scales))
 
         for n in range(FLIP_AHEAD):
-            flip_x(n)
+            flip_x(banks, n)
         for n in range(QUANT_AHEAD):
             quantise_x(n)
 
@@ -116,10 +118,11 @@ def tile_internattention_pa_t_kernel(
             for half in range(2):
                 words = slice(half * 2 * WORDS, (half + 1) * 2 * WORDS)
                 flip(
+                    banks,
                     w_raw[c][:].bitcast(F32)[:, words],
                     w_grouped[:].bitcast(F32)[:, words],
                     2,
-                    nc.scalar.copy,
+                    (nc.scalar.copy, nc.vector.tensor_copy)[half],
                 )
             w_codes = w_pool.tile([P, HIDDEN], U32, align_bytes=64)
             w_scales = w_pool.tile([P, HIDDEN], U8, align_bytes=64)
@@ -130,7 +133,7 @@ def tile_internattention_pa_t_kernel(
 
         gains = consts.tile([P, 2, HIDDEN], F32)
         for c in range(2):
-            spread = psum.tile([P, HIDDEN], F32, tag="acc_v")
+            spread = banks.tile([P, HIDDEN], F32, tag="bank")
             nc.tensor.matmul(
                 out=spread[:],
                 lhsT=ones[:],
@@ -138,7 +141,7 @@ def tile_internattention_pa_t_kernel(
                 start=True,
                 stop=True,
             )
-            nc.scalar.copy(out=gains[:, c, :], in_=spread[:])
+            (nc.scalar.copy, nc.vector.tensor_copy)[c](out=gains[:, c, :], in_=spread[:])
 
         for n in range(TILES):
             b = n % STORED
@@ -159,11 +162,11 @@ def tile_internattention_pa_t_kernel(
                     stop=True,
                 )
 
-            acc_q = psum.tile([P, HIDDEN], F32)
+            acc_q = banks.tile([P, HIDDEN], F32, tag="bank")
             project(acc_q, 0)
-            acc_k = psum.tile([P, HIDDEN], F32)
+            acc_k = banks.tile([P, HIDDEN], F32, tag="bank")
             project(acc_k, 1)
-            acc_v = psum.tile([P, HIDDEN], F32)
+            acc_v = banks.tile([P, HIDDEN], F32, tag="bank")
             project(acc_v, 2)
 
             sum_sq = small.tile([P, 2], F32)
@@ -175,14 +178,17 @@ def tile_internattention_pa_t_kernel(
             nc.scalar.activation(
                 out=squares[:], in_=acc_k[:], func=ACT.Square, accum_out=sum_sq[:, 1:2]
             )
+            nc.scalar.copy(out=v_out[:, b, :], in_=acc_v[:])
             rms = small.tile([P, 2], F32)
             nc.scalar.activation(
                 out=rms[:], in_=sum_sq[:], func=ACT.Sqrt, scale=1.0 / HIDDEN, bias=eps[:]
             )
-            nc.scalar.copy(out=v_out[:, b, :], in_=acc_v[:])
-
             inv_rms = small.tile([P, 2], F32)
             nc.vector.reciprocal(out=inv_rms[:], in_=rms[:])
+            if n + FLIP_AHEAD < TILES:
+                flip_x(flip_bank, n + FLIP_AHEAD)
+            if n + QUANT_AHEAD < TILES:
+                quantise_x(n + QUANT_AHEAD)
             nc.vector.scalar_tensor_tensor(
                 out=q_out[:, b, :],
                 in0=acc_q[:],
@@ -199,11 +205,6 @@ def tile_internattention_pa_t_kernel(
                 op0=ALU.mult,
                 op1=ALU.mult,
             )
-
-            if n + FLIP_AHEAD < TILES:
-                flip_x(n + FLIP_AHEAD)
-            if n + QUANT_AHEAD < TILES:
-                quantise_x(n + QUANT_AHEAD)
 
             if b == STORED - 1:
                 tiles = slice(n + 1 - STORED, n + 1)

@@ -36,8 +36,10 @@ def tile_internattention_pa_t_kernel(
         w_pool = ctx.enter_context(tc.tile_pool(name="w_pool", bufs=3))
         x_mx_pool = ctx.enter_context(tc.tile_pool(name="x_mx_pool", bufs=FLIP_AHEAD + 2))
         small = ctx.enter_context(tc.tile_pool(name="small", bufs=4))
-        out_pool = ctx.enter_context(tc.tile_pool(name="out_pool", bufs=8))
-        banks = ctx.enter_context(tc.psum_pool(name="banks", bufs=7))
+        out_pool = ctx.enter_context(tc.tile_pool(name="out_pool", bufs=5))
+        q_banks = ctx.enter_context(tc.psum_pool(name="q_banks", bufs=3))
+        k_banks = ctx.enter_context(tc.psum_pool(name="k_banks", bufs=3))
+        v_bank = ctx.enter_context(tc.psum_pool(name="v_bank", bufs=1))
         flip_bank = ctx.enter_context(tc.psum_pool(name="flip_bank", bufs=1))
         ctx.enter_context(tc.manual_schedule())
 
@@ -45,20 +47,18 @@ def tile_internattention_pa_t_kernel(
         q_rows = out_0.flatten_outer_dims().rearrange("(p t) c -> p t c", t=TILES)
         k_rows = out_1.flatten_outer_dims().rearrange("(p t) c -> p t c", t=TILES)
         v_rows = out_2.flatten_outer_dims().rearrange("(p t) c -> p t c", t=TILES)
-        w_rows = w_qkv.rearrange("(j p) k -> p j k", p=P)
+        w_rows = w_qkv.rearrange("(c p j) k -> c p j k", c=3, j=BLOCKS)
 
         gain_rows = consts.tile([P, 2 * HIDDEN], BF16)
         nc.vector.memset(gain_rows[:], 0.0)
         ones = consts.tile([P, P], BF16)
         nc.vector.memset(ones[:], 1.0)
-        eps = consts.tile([P, 1], F32)
-        nc.vector.memset(eps[:], EPS)
+        minus_half = consts.tile([P, 2], F32)
+        nc.vector.memset(minus_half[:], -0.5)
         ident = consts.tile([P, P], F32)
         make_identity(nc, ident[:])
         nc.scalar.dma_start(out=gain_rows[0:1, 0:HIDDEN], in_=q_norm_w.unsqueeze(0))
         nc.scalar.dma_start(out=gain_rows[0:1, HIDDEN : 2 * HIDDEN], in_=k_norm_w.unsqueeze(0))
-        warm = consts.tile([P, 1], F32)
-        nc.scalar.activation(out=warm[:], in_=eps[:], func=ACT.Sqrt)
 
         def load(pool, rows):
             raw = pool.tile([P, BLOCKS * HIDDEN], BF16)
@@ -66,7 +66,7 @@ def tile_internattention_pa_t_kernel(
             return raw
 
         x_raw = [load(x_pool, x_rows[:, 0:BLOCKS, :])]
-        w_raw = [load(w_pool, w_rows[:, c * BLOCKS : (c + 1) * BLOCKS, :]) for c in range(3)]
+        w_raw = [load(w_pool, w_rows[c]) for c in range(3)]
         for g in range(1, GROUPS):
             x_raw.append(load(x_pool, x_rows[:, g * BLOCKS : (g + 1) * BLOCKS, :]))
 
@@ -80,8 +80,8 @@ def tile_internattention_pa_t_kernel(
                         identity=ident[:],
                     )
             copy(
-                out=grouped_words.rearrange("p (b r u) -> p b r u", b=blocks, u=2),
-                in_=flipped[:].rearrange("p (b u r) -> p b r u", b=blocks, u=2),
+                out=grouped_words,
+                in_=flipped[:].rearrange("p (b u r) -> p r b u", b=blocks, u=2),
             )
 
         x_grouped = []
@@ -93,7 +93,7 @@ def tile_internattention_pa_t_kernel(
             flip(
                 pool,
                 x_raw[g][:].bitcast(F32)[:, b * WORDS : (b + 1) * WORDS],
-                grouped[:].bitcast(F32),
+                grouped[:].bitcast(F32).rearrange("p (r b u) -> p r b u", b=1, u=2),
                 1,
                 nc.vector.tensor_copy,
             )
@@ -108,21 +108,23 @@ def tile_internattention_pa_t_kernel(
             x_mx.append((x_codes, x_scales))
 
         for n in range(FLIP_AHEAD):
-            flip_x(banks, n)
+            flip_x((q_banks, k_banks)[n % 2], n)
         for n in range(QUANT_AHEAD):
             quantise_x(n)
 
         w_mx = []
         for c in range(3):
             w_grouped = w_pool.tile([P, BLOCKS * HIDDEN], BF16, align_bytes=64)
-            for half in range(2):
-                words = slice(half * 2 * WORDS, (half + 1) * 2 * WORDS)
+            w_grouped_words = w_grouped[:].bitcast(F32).rearrange(
+                "p (r h b u) -> p h r b u", h=2, b=2, u=2
+            )
+            for h in range(2):
                 flip(
-                    banks,
-                    w_raw[c][:].bitcast(F32)[:, words],
-                    w_grouped[:].bitcast(F32)[:, words],
+                    (q_banks, k_banks)[h],
+                    w_raw[c][:].bitcast(F32)[:, h * 2 * WORDS : (h + 1) * 2 * WORDS],
+                    w_grouped_words[:, h],
                     2,
-                    (nc.scalar.copy, nc.vector.tensor_copy)[half],
+                    (nc.scalar.copy, nc.vector.tensor_copy)[c % 2],
                 )
             w_codes = w_pool.tile([P, HIDDEN], U32, align_bytes=64)
             w_scales = w_pool.tile([P, HIDDEN], U8, align_bytes=64)
@@ -133,7 +135,7 @@ def tile_internattention_pa_t_kernel(
 
         gains = consts.tile([P, 2, HIDDEN], F32)
         for c in range(2):
-            spread = banks.tile([P, HIDDEN], F32, tag="bank")
+            spread = (q_banks, k_banks)[c].tile([P, HIDDEN], F32, tag="bank")
             nc.tensor.matmul(
                 out=spread[:],
                 lhsT=ones[:],
@@ -143,55 +145,62 @@ def tile_internattention_pa_t_kernel(
             )
             (nc.scalar.copy, nc.vector.tensor_copy)[c](out=gains[:, c, :], in_=spread[:])
 
+        def project(pool, n, c):
+            acc = pool.tile([P, HIDDEN], F32, tag="bank")
+            nc.tensor.matmul_mx(
+                out=acc[:],
+                lhsT=x_mx[n][0][:].bitcast(FP8X4),
+                lhsT_scale=x_mx[n][1][:],
+                rhs=w_mx[c][0][:].bitcast(FP8X4),
+                rhs_scale=w_mx[c][1][:],
+                start=True,
+                stop=True,
+            )
+            return acc
+
+        acc_q = [project(q_banks, 0, 0)]
+        acc_k = [project(k_banks, 0, 1)]
         for n in range(TILES):
-            b = n % STORED
+            g, b = divmod(n, BLOCKS)
             if b == 0:
-                q_out = out_pool.tile([P, STORED, HIDDEN], F32)
-                k_out = out_pool.tile([P, STORED, HIDDEN], F32)
-                v_out = out_pool.tile([P, STORED, HIDDEN], F32)
-            x_codes, x_scales = x_mx[n]
-
-            def project(acc, c):
-                nc.tensor.matmul_mx(
-                    out=acc[:],
-                    lhsT=x_codes[:].bitcast(FP8X4),
-                    lhsT_scale=x_scales[:],
-                    rhs=w_mx[c][0][:].bitcast(FP8X4),
-                    rhs_scale=w_mx[c][1][:],
-                    start=True,
-                    stop=True,
-                )
-
-            acc_q = banks.tile([P, HIDDEN], F32, tag="bank")
-            project(acc_q, 0)
-            acc_k = banks.tile([P, HIDDEN], F32, tag="bank")
-            project(acc_k, 1)
-            acc_v = banks.tile([P, HIDDEN], F32, tag="bank")
-            project(acc_v, 2)
+                q_out = out_pool.tile([P, BLOCKS, HIDDEN], F32)
+                k_out = out_pool.tile([P, BLOCKS, HIDDEN], F32)
+                v_out = out_pool.tile([P, BLOCKS, HIDDEN], F32)
+            acc_v = project(v_bank, n, 2)
+            if n + 1 < TILES:
+                acc_q.append(project(q_banks, n + 1, 0))
+                acc_k.append(project(k_banks, n + 1, 1))
 
             sum_sq = small.tile([P, 2], F32)
             squares = small.tile([P, HIDDEN], BF16)
             nc.scalar.activation(
-                out=squares[:], in_=acc_q[:], func=ACT.Square, accum_out=sum_sq[:, 0:1]
+                out=squares[:], in_=acc_q[n][:], func=ACT.Square, accum_out=sum_sq[:, 0:1]
             )
             squares = small.tile([P, HIDDEN], BF16)
             nc.scalar.activation(
-                out=squares[:], in_=acc_k[:], func=ACT.Square, accum_out=sum_sq[:, 1:2]
+                out=squares[:], in_=acc_k[n][:], func=ACT.Square, accum_out=sum_sq[:, 1:2]
             )
             nc.scalar.copy(out=v_out[:, b, :], in_=acc_v[:])
-            rms = small.tile([P, 2], F32)
-            nc.scalar.activation(
-                out=rms[:], in_=sum_sq[:], func=ACT.Sqrt, scale=1.0 / HIDDEN, bias=eps[:]
+
+            mean_sq = small.tile([P, 2], F32)
+            nc.gpsimd.tensor_scalar(
+                out=mean_sq[:],
+                in0=sum_sq[:],
+                scalar1=1.0 / HIDDEN,
+                scalar2=EPS,
+                op0=ALU.mult,
+                op1=ALU.add,
             )
             inv_rms = small.tile([P, 2], F32)
-            nc.vector.reciprocal(out=inv_rms[:], in_=rms[:])
+            nc.gpsimd.tensor_tensor(out=inv_rms[:], in0=mean_sq[:], in1=minus_half[:], op=ALU.pow)
+
             if n + FLIP_AHEAD < TILES:
                 flip_x(flip_bank, n + FLIP_AHEAD)
             if n + QUANT_AHEAD < TILES:
                 quantise_x(n + QUANT_AHEAD)
             nc.vector.scalar_tensor_tensor(
                 out=q_out[:, b, :],
-                in0=acc_q[:],
+                in0=acc_q[n][:],
                 scalar=inv_rms[:, 0:1],
                 in1=gains[:, 0, :],
                 op0=ALU.mult,
@@ -199,15 +208,17 @@ def tile_internattention_pa_t_kernel(
             )
             nc.vector.scalar_tensor_tensor(
                 out=k_out[:, b, :],
-                in0=acc_k[:],
+                in0=acc_k[n][:],
                 scalar=inv_rms[:, 1:2],
                 in1=gains[:, 1, :],
                 op0=ALU.mult,
                 op1=ALU.mult,
             )
 
-            if b == STORED - 1:
-                tiles = slice(n + 1 - STORED, n + 1)
-                nc.sync.dma_start(out=v_rows[:, tiles, :], in_=v_out[:])
-                nc.sync.dma_start(out=q_rows[:, tiles, :], in_=q_out[:])
-                nc.sync.dma_start(out=k_rows[:, tiles, :], in_=k_out[:])
+            step = STORED
+            if (b + 1) % step == 0:
+                part = slice(b + 1 - step, b + 1)
+                tiles = slice(n + 1 - step, n + 1)
+                nc.sync.dma_start(out=v_rows[:, tiles, :], in_=v_out[:, part, :])
+                nc.sync.dma_start(out=q_rows[:, tiles, :], in_=q_out[:, part, :])
+                nc.sync.dma_start(out=k_rows[:, tiles, :], in_=k_out[:, part, :])

@@ -17,11 +17,11 @@ TOKENS = 4 * 1024
 TILES = TOKENS // P
 BLOCKS = 4
 GROUPS = TILES // BLOCKS
-STORED = 2
+VECTOR_V = 6
 WORDS = HIDDEN // 2
 EPS = 1e-6
-FLIP_AHEAD = 4
-QUANT_AHEAD = 3
+FLIP_AHEAD = 6
+QUANT_AHEAD = 5
 
 FLOPS = 2 * TOKENS * HIDDEN * 3 * HIDDEN
 
@@ -34,11 +34,11 @@ def tile_internattention_pa_t_kernel(
         consts = ctx.enter_context(tc.tile_pool(name="consts", bufs=1))
         x_pool = ctx.enter_context(tc.tile_pool(name="x_pool", bufs=GROUPS))
         w_pool = ctx.enter_context(tc.tile_pool(name="w_pool", bufs=3))
-        x_mx_pool = ctx.enter_context(tc.tile_pool(name="x_mx_pool", bufs=FLIP_AHEAD + 2))
+        x_mx_pool = ctx.enter_context(tc.tile_pool(name="x_mx_pool", bufs=2 * FLIP_AHEAD))
         small = ctx.enter_context(tc.tile_pool(name="small", bufs=4))
         out_pool = ctx.enter_context(tc.tile_pool(name="out_pool", bufs=5))
-        q_banks = ctx.enter_context(tc.psum_pool(name="q_banks", bufs=3))
-        k_banks = ctx.enter_context(tc.psum_pool(name="k_banks", bufs=3))
+        a_banks = ctx.enter_context(tc.psum_pool(name="a_banks", bufs=3))
+        b_banks = ctx.enter_context(tc.psum_pool(name="b_banks", bufs=3))
         v_bank = ctx.enter_context(tc.psum_pool(name="v_bank", bufs=1))
         flip_bank = ctx.enter_context(tc.psum_pool(name="flip_bank", bufs=1))
         ctx.enter_context(tc.manual_schedule())
@@ -107,9 +107,9 @@ def tile_internattention_pa_t_kernel(
             )
             x_mx.append((x_codes, x_scales))
 
-        for n in range(FLIP_AHEAD):
-            flip_x((q_banks, k_banks)[n % 2], n)
-        for n in range(QUANT_AHEAD):
+        for n in range(BLOCKS):
+            flip_x((a_banks, b_banks)[n % 2], n)
+        for n in range(BLOCKS):
             quantise_x(n)
 
         w_mx = []
@@ -120,7 +120,7 @@ def tile_internattention_pa_t_kernel(
             )
             for h in range(2):
                 flip(
-                    (q_banks, k_banks)[h],
+                    (a_banks, b_banks)[h],
                     w_raw[c][:].bitcast(F32)[:, h * 2 * WORDS : (h + 1) * 2 * WORDS],
                     w_grouped_words[:, h],
                     2,
@@ -135,7 +135,7 @@ def tile_internattention_pa_t_kernel(
 
         gains = consts.tile([P, 2, HIDDEN], F32)
         for c in range(2):
-            spread = (q_banks, k_banks)[c].tile([P, HIDDEN], F32, tag="bank")
+            spread = (a_banks, b_banks)[c].tile([P, HIDDEN], F32, tag="bank")
             nc.tensor.matmul(
                 out=spread[:],
                 lhsT=ones[:],
@@ -144,6 +144,11 @@ def tile_internattention_pa_t_kernel(
                 stop=True,
             )
             (nc.scalar.copy, nc.vector.tensor_copy)[c](out=gains[:, c, :], in_=spread[:])
+
+        for n in range(BLOCKS, FLIP_AHEAD):
+            flip_x((a_banks, b_banks)[n % 2], n)
+        for n in range(BLOCKS, QUANT_AHEAD):
+            quantise_x(n)
 
         def project(pool, n, c):
             acc = pool.tile([P, HIDDEN], F32, tag="bank")
@@ -158,29 +163,41 @@ def tile_internattention_pa_t_kernel(
             )
             return acc
 
-        acc_q = [project(q_banks, 0, 0)]
-        acc_k = [project(k_banks, 0, 1)]
-        for n in range(TILES):
-            g, b = divmod(n, BLOCKS)
-            if b == 0:
+        def norm_pair(m):
+            g, s = divmod(m, BLOCKS)
+            return s // 2, g * BLOCKS + 2 * (s % 2)
+
+        def project_pair(m):
+            c, n = norm_pair(m)
+            return project(a_banks, n, c), project(b_banks, n + 1, c)
+
+        def vector_copies_v(m):
+            return m < TILES and m % VECTOR_V == VECTOR_V - 1
+
+        pairs = [project_pair(0)]
+        for m in range(TILES):
+            g, s = divmod(m, BLOCKS)
+            if s == 0:
                 q_out = out_pool.tile([P, BLOCKS, HIDDEN], F32)
                 k_out = out_pool.tile([P, BLOCKS, HIDDEN], F32)
                 v_out = out_pool.tile([P, BLOCKS, HIDDEN], F32)
-            acc_v = project(v_bank, n, 2)
-            if n + 1 < TILES:
-                acc_q.append(project(q_banks, n + 1, 0))
-                acc_k.append(project(k_banks, n + 1, 1))
+            if not vector_copies_v(m):
+                acc_v = project(v_bank, m, 2)
+            if m + 1 < TILES:
+                pairs.append(project_pair(m + 1))
+            acc_a, acc_b = pairs[m]
 
             sum_sq = small.tile([P, 2], F32)
             squares = small.tile([P, HIDDEN], BF16)
             nc.scalar.activation(
-                out=squares[:], in_=acc_q[n][:], func=ACT.Square, accum_out=sum_sq[:, 0:1]
+                out=squares[:], in_=acc_a[:], func=ACT.Square, accum_out=sum_sq[:, 0:1]
             )
             squares = small.tile([P, HIDDEN], BF16)
             nc.scalar.activation(
-                out=squares[:], in_=acc_k[n][:], func=ACT.Square, accum_out=sum_sq[:, 1:2]
+                out=squares[:], in_=acc_b[:], func=ACT.Square, accum_out=sum_sq[:, 1:2]
             )
-            nc.scalar.copy(out=v_out[:, b, :], in_=acc_v[:])
+            if not vector_copies_v(m):
+                nc.scalar.copy(out=v_out[:, s, :], in_=acc_v[:])
 
             mean_sq = small.tile([P, 2], F32)
             nc.gpsimd.tensor_scalar(
@@ -194,31 +211,28 @@ def tile_internattention_pa_t_kernel(
             inv_rms = small.tile([P, 2], F32)
             nc.gpsimd.tensor_tensor(out=inv_rms[:], in0=mean_sq[:], in1=minus_half[:], op=ALU.pow)
 
-            if n + FLIP_AHEAD < TILES:
-                flip_x(flip_bank, n + FLIP_AHEAD)
-            if n + QUANT_AHEAD < TILES:
-                quantise_x(n + QUANT_AHEAD)
-            nc.vector.scalar_tensor_tensor(
-                out=q_out[:, b, :],
-                in0=acc_q[n][:],
-                scalar=inv_rms[:, 0:1],
-                in1=gains[:, 0, :],
-                op0=ALU.mult,
-                op1=ALU.mult,
-            )
-            nc.vector.scalar_tensor_tensor(
-                out=k_out[:, b, :],
-                in0=acc_k[n][:],
-                scalar=inv_rms[:, 1:2],
-                in1=gains[:, 1, :],
-                op0=ALU.mult,
-                op1=ALU.mult,
-            )
+            if m + FLIP_AHEAD < TILES:
+                flip_x(flip_bank, m + FLIP_AHEAD)
+            if m + QUANT_AHEAD < TILES:
+                quantise_x(m + QUANT_AHEAD)
+            if vector_copies_v(m + 1):
+                acc_v = project(v_bank, m + 1, 2)
+                nc.vector.tensor_copy(out=v_out[:, s + 1, :], in_=acc_v[:])
+            c, n = norm_pair(m)
+            normed = (q_out, k_out)[c]
+            for i, acc in enumerate((acc_a, acc_b)):
+                nc.vector.scalar_tensor_tensor(
+                    out=normed[:, n % BLOCKS + i, :],
+                    in0=acc[:],
+                    scalar=inv_rms[:, i : i + 1],
+                    in1=gains[:, c, :],
+                    op0=ALU.mult,
+                    op1=ALU.mult,
+                )
 
-            step = STORED
-            if (b + 1) % step == 0:
-                part = slice(b + 1 - step, b + 1)
-                tiles = slice(n + 1 - step, n + 1)
-                nc.sync.dma_start(out=v_rows[:, tiles, :], in_=v_out[:, part, :])
-                nc.sync.dma_start(out=q_rows[:, tiles, :], in_=q_out[:, part, :])
-                nc.sync.dma_start(out=k_rows[:, tiles, :], in_=k_out[:, part, :])
+            tiles = slice(g * BLOCKS, (g + 1) * BLOCKS)
+            if s == 1:
+                nc.sync.dma_start(out=q_rows[:, tiles, :], in_=q_out[:])
+            if s == BLOCKS - 1:
+                nc.sync.dma_start(out=v_rows[:, tiles, :], in_=v_out[:])
+                nc.sync.dma_start(out=k_rows[:, tiles, :], in_=k_out[:])

from contextlib import ExitStack

import concourse.mybir as mybir
from concourse.masks import make_identity

F32 = mybir.dt.float32
BF16 = mybir.dt.bfloat16
U32 = mybir.dt.uint32
U8 = mybir.dt.uint8
FP8X4 = mybir.dt.float8_e4m3fn_x4
ACT = mybir.ActivationFunctionType
ALU = mybir.AluOpType

P = 128
HIDDEN = 512
TOKENS = 4 * 1024
TILES = TOKENS // P
BLOCKS = 4
GROUPS = TILES // BLOCKS
VECTOR_V = 6
WORDS = HIDDEN // 2
EPS = 1e-6
FLIP_AHEAD = 6
QUANT_AHEAD = 5

FLOPS = 2 * TOKENS * HIDDEN * 3 * HIDDEN


def tile_internattention_pa_t_kernel(
    tc, x, w_qkv, q_norm_w, k_norm_w, out_0, out_1, out_2
):
    nc = tc.nc
    with ExitStack() as ctx:
        consts = ctx.enter_context(tc.tile_pool(name="consts", bufs=1))
        x_pool = ctx.enter_context(tc.tile_pool(name="x_pool", bufs=GROUPS))
        w_pool = ctx.enter_context(tc.tile_pool(name="w_pool", bufs=3))
        x_mx_pool = ctx.enter_context(tc.tile_pool(name="x_mx_pool", bufs=2 * FLIP_AHEAD))
        small = ctx.enter_context(tc.tile_pool(name="small", bufs=4))
        out_pool = ctx.enter_context(tc.tile_pool(name="out_pool", bufs=5))
        a_banks = ctx.enter_context(tc.psum_pool(name="a_banks", bufs=3))
        b_banks = ctx.enter_context(tc.psum_pool(name="b_banks", bufs=3))
        v_bank = ctx.enter_context(tc.psum_pool(name="v_bank", bufs=1))
        flip_bank = ctx.enter_context(tc.psum_pool(name="flip_bank", bufs=1))
        ctx.enter_context(tc.manual_schedule())

        x_rows = x.flatten_outer_dims().rearrange("(p t) k -> p t k", t=TILES)
        q_rows = out_0.flatten_outer_dims().rearrange("(p t) c -> p t c", t=TILES)
        k_rows = out_1.flatten_outer_dims().rearrange("(p t) c -> p t c", t=TILES)
        v_rows = out_2.flatten_outer_dims().rearrange("(p t) c -> p t c", t=TILES)
        w_rows = w_qkv.rearrange("(c p j) k -> c p j k", c=3, j=BLOCKS)

        gain_rows = consts.tile([P, 2 * HIDDEN], BF16)
        nc.vector.memset(gain_rows[:], 0.0)
        ones = consts.tile([P, P], BF16)
        nc.vector.memset(ones[:], 1.0)
        minus_half = consts.tile([P, 2], F32)
        nc.vector.memset(minus_half[:], -0.5)
        ident = consts.tile([P, P], F32)
        make_identity(nc, ident[:])
        nc.scalar.dma_start(out=gain_rows[0:1, 0:HIDDEN], in_=q_norm_w.unsqueeze(0))
        nc.scalar.dma_start(out=gain_rows[0:1, HIDDEN : 2 * HIDDEN], in_=k_norm_w.unsqueeze(0))

        def load(pool, rows):
            raw = pool.tile([P, BLOCKS * HIDDEN], BF16)
            nc.sync.dma_start(out=raw[:].rearrange("p (b k) -> p b k", b=BLOCKS), in_=rows)
            return raw

        x_raw = [load(x_pool, x_rows[:, 0:BLOCKS, :])]
        w_raw = [load(w_pool, w_rows[c]) for c in range(3)]
        for g in range(1, GROUPS):
            x_raw.append(load(x_pool, x_rows[:, g * BLOCKS : (g + 1) * BLOCKS, :]))

        def flip(pool, raw_words, grouped_words, blocks, copy):
            flipped = pool.tile([P, blocks * WORDS], F32, tag="bank")
            for b in range(blocks):
                for u in range(2):
                    nc.tensor.transpose(
                        out=flipped[:, (2 * b + u) * P : (2 * b + u + 1) * P],
                        in_=raw_words[:, b * WORDS + u * P : b * WORDS + (u + 1) * P],
                        identity=ident[:],
                    )
            copy(
                out=grouped_words,
                in_=flipped[:].rearrange("p (b u r) -> p r b u", b=blocks, u=2),
            )

        x_grouped = []
        x_mx = []

        def flip_x(pool, n):
            g, b = divmod(n, BLOCKS)
            grouped = x_mx_pool.tile([P, HIDDEN], BF16, align_bytes=64)
            flip(
                pool,
                x_raw[g][:].bitcast(F32)[:, b * WORDS : (b + 1) * WORDS],
                grouped[:].bitcast(F32).rearrange("p (r b u) -> p r b u", b=1, u=2),
                1,
                nc.vector.tensor_copy,
            )
            x_grouped.append(grouped)

        def quantise_x(n):
            x_codes = x_mx_pool.tile([P, P], U32, align_bytes=64)
            x_scales = x_mx_pool.tile([P, P], U8, align_bytes=64)
            nc.vector.quantize_mx(
                out=x_codes[:].bitcast(FP8X4), scales=x_scales[:], in_=x_grouped[n][:]
            )
            x_mx.append((x_codes, x_scales))

        for n in range(BLOCKS):
            flip_x((a_banks, b_banks)[n % 2], n)
        for n in range(BLOCKS):
            quantise_x(n)

        w_mx = []
        for c in range(3):
            w_grouped = w_pool.tile([P, BLOCKS * HIDDEN], BF16, align_bytes=64)
            w_grouped_words = w_grouped[:].bitcast(F32).rearrange(
                "p (r h b u) -> p h r b u", h=2, b=2, u=2
            )
            for h in range(2):
                flip(
                    (a_banks, b_banks)[h],
                    w_raw[c][:].bitcast(F32)[:, h * 2 * WORDS : (h + 1) * 2 * WORDS],
                    w_grouped_words[:, h],
                    2,
                    (nc.scalar.copy, nc.vector.tensor_copy)[c % 2],
                )
            w_codes = w_pool.tile([P, HIDDEN], U32, align_bytes=64)
            w_scales = w_pool.tile([P, HIDDEN], U8, align_bytes=64)
            nc.vector.quantize_mx(
                out=w_codes[:].bitcast(FP8X4), scales=w_scales[:], in_=w_grouped[:]
            )
            w_mx.append((w_codes, w_scales))

        gains = consts.tile([P, 2, HIDDEN], F32)
        for c in range(2):
            spread = (a_banks, b_banks)[c].tile([P, HIDDEN], F32, tag="bank")
            nc.tensor.matmul(
                out=spread[:],
                lhsT=ones[:],
                rhs=gain_rows[:, c * HIDDEN : (c + 1) * HIDDEN],
                start=True,
                stop=True,
            )
            (nc.scalar.copy, nc.vector.tensor_copy)[c](out=gains[:, c, :], in_=spread[:])

        for n in range(BLOCKS, FLIP_AHEAD):
            flip_x((a_banks, b_banks)[n % 2], n)
        for n in range(BLOCKS, QUANT_AHEAD):
            quantise_x(n)

        def project(pool, n, c):
            acc = pool.tile([P, HIDDEN], F32, tag="bank")
            nc.tensor.matmul_mx(
                out=acc[:],
                lhsT=x_mx[n][0][:].bitcast(FP8X4),
                lhsT_scale=x_mx[n][1][:],
                rhs=w_mx[c][0][:].bitcast(FP8X4),
                rhs_scale=w_mx[c][1][:],
                start=True,
                stop=True,
            )
            return acc

        def norm_pair(m):
            g, s = divmod(m, BLOCKS)
            return s // 2, g * BLOCKS + 2 * (s % 2)

        def project_pair(m):
            c, n = norm_pair(m)
            return project(a_banks, n, c), project(b_banks, n + 1, c)

        def vector_copies_v(m):
            return m < TILES and m % VECTOR_V == VECTOR_V - 1

        pairs = [project_pair(0)]
        for m in range(TILES):
            g, s = divmod(m, BLOCKS)
            if s == 0:
                q_out = out_pool.tile([P, BLOCKS, HIDDEN], F32)
                k_out = out_pool.tile([P, BLOCKS, HIDDEN], F32)
                v_out = out_pool.tile([P, BLOCKS, HIDDEN], F32)
            if not vector_copies_v(m):
                acc_v = project(v_bank, m, 2)
            if m + 1 < TILES:
                pairs.append(project_pair(m + 1))
            acc_a, acc_b = pairs[m]

            sum_sq = small.tile([P, 2], F32)
            squares = small.tile([P, HIDDEN], BF16)
            nc.scalar.activation(
                out=squares[:], in_=acc_a[:], func=ACT.Square, accum_out=sum_sq[:, 0:1]
            )
            squares = small.tile([P, HIDDEN], BF16)
            nc.scalar.activation(
                out=squares[:], in_=acc_b[:], func=ACT.Square, accum_out=sum_sq[:, 1:2]
            )
            if not vector_copies_v(m):
                nc.scalar.copy(out=v_out[:, s, :], in_=acc_v[:])

            mean_sq = small.tile([P, 2], F32)
            nc.gpsimd.tensor_scalar(
                out=mean_sq[:],
                in0=sum_sq[:],
                scalar1=1.0 / HIDDEN,
                scalar2=EPS,
                op0=ALU.mult,
                op1=ALU.add,
            )
            inv_rms = small.tile([P, 2], F32)
            nc.gpsimd.tensor_tensor(out=inv_rms[:], in0=mean_sq[:], in1=minus_half[:], op=ALU.pow)

            if m + FLIP_AHEAD < TILES:
                flip_x(flip_bank, m + FLIP_AHEAD)
            if m + QUANT_AHEAD < TILES:
                quantise_x(m + QUANT_AHEAD)
            if vector_copies_v(m + 1):
                acc_v = project(v_bank, m + 1, 2)
                nc.vector.tensor_copy(out=v_out[:, s + 1, :], in_=acc_v[:])
            c, n = norm_pair(m)
            normed = (q_out, k_out)[c]
            for i, acc in enumerate((acc_a, acc_b)):
                nc.vector.scalar_tensor_tensor(
                    out=normed[:, n % BLOCKS + i, :],
                    in0=acc[:],
                    scalar=inv_rms[:, i : i + 1],
                    in1=gains[:, c, :],
                    op0=ALU.mult,
                    op1=ALU.mult,
                )

            tiles = slice(g * BLOCKS, (g + 1) * BLOCKS)
            if s == 1:
                nc.sync.dma_start(out=q_rows[:, tiles, :], in_=q_out[:])
            if s == BLOCKS - 1:
                nc.sync.dma_start(out=v_rows[:, tiles, :], in_=v_out[:])
                nc.sync.dma_start(out=k_rows[:, tiles, :], in_=k_out[:])
